import numpy as np
import ml_dtypes


def mxq(x, axis, fmt="e4m3"):
    dtype, down = {"e4m3": (ml_dtypes.float8_e4m3fn, 7), "e5m2": (ml_dtypes.float8_e5m2, 14)}[fmt]
    v = np.moveaxis(np.asarray(x, np.float32).astype(ml_dtypes.bfloat16).astype(np.float64), axis, -1)
    blocks = v.reshape(v.shape[:-1] + (-1, 32))
    amax = np.abs(blocks).max(-1, keepdims=True)
    byte = np.maximum(np.where(amax > 0, np.frexp(amax)[1] - 1 + 127, 0) - down, 1)
    scale = np.exp2(byte - 127.0)
    codes = (blocks / scale).astype(np.float32).astype(dtype).astype(np.float64)
    return np.moveaxis((codes * scale).reshape(v.shape), -1, axis)


WIDE = False


def mx_kscale(k):
    if not WIDE:
        return np.ones(k)
    levels = np.array([10, -10, 5, -5, 0])
    a = np.random.permutation(np.resize(levels, k // 512 * 4)).reshape(k // 512, 4)
    idx = np.arange(k)
    return np.exp2(a[idx // 512, idx % 128 // 32])


BF16 = ml_dtypes.bfloat16


def bf(x):
    return np.asarray(x, np.float32).astype(BF16)


def f64(x):
    return np.asarray(x).astype(np.float64)


E2M1 = np.array([0.0, 0.5, 1.0, 1.5, 2.0, 3.0, 4.0, 6.0, -0.0, -0.5, -1.0, -1.5, -2.0, -3.0, -4.0, -6.0])


def pack_weight(w, fmt):
    k, n = w.shape
    w = f64(bf(w)).reshape(k // 32, 32, n)
    amax = np.abs(w).max(1)
    if fmt == "e4m3":
        byte = np.frexp(amax)[1] - 1 + 127 - 7
    else:
        mant, ex = np.frexp(amax / 6.0)
        byte = np.where(mant > 0.5, ex, ex - 1) + 127
    byte = np.clip(np.where(amax > 0, byte, 1), 1, 254)
    scaled = (w * np.exp2(127.0 - byte)[:, None, :]).reshape(k, n).astype(np.float32)
    by_word = np.ascontiguousarray(scaled.reshape(k // 512, 128, 4, n).transpose(0, 1, 3, 2))
    if fmt == "e4m3":
        words = by_word.astype(ml_dtypes.float8_e4m3fn).view(np.uint8)
    else:
        c = by_word.astype(ml_dtypes.float4_e2m1fn).view(np.uint8) & 0xF
        words = c[..., 0::2] | (c[..., 1::2] << 4)
    return np.ascontiguousarray(words), np.ascontiguousarray(byte.astype(np.uint8).reshape(k // 512, 16, n))


def unpack_weight(words, scales, fmt):
    g, p, n, _ = words.shape
    if fmt == "e4m3":
        vals = np.ascontiguousarray(words).view(ml_dtypes.float8_e4m3fn).astype(np.float64)
    else:
        nib = np.empty((g, p, n, 4), np.uint8)
        nib[..., 0::2] = words & 0xF
        nib[..., 1::2] = words >> 4
        vals = E2M1[nib]
    vals = vals * np.repeat(np.exp2(scales.astype(np.float64) - 127.0), 8, axis=1)[..., None]
    return vals.transpose(0, 1, 3, 2).reshape(g * 512, n)


B, L, D, DV, BN = 2, 512, 8192, 256, 64
SV = 2.0 * B / np.sqrt(L)
SB = 2.0 * B / L


def setup_inputs():
    s, u = mx_kscale(D), mx_kscale(D)
    qp_top = bf(np.random.standard_normal((B, BN, D)) * s)
    kp = bf(np.random.standard_normal((B, L, D)) / s)
    v = bf(np.random.standard_normal((B, L, D)) * u)
    Wv = np.random.standard_normal((DV, D)) * SV / np.sqrt(D) / u[None, :]
    Wv_words, Wv_scales = pack_weight(np.ascontiguousarray(Wv.T), "e4m3")
    bv = bf(np.random.standard_normal(DV) * SB)
    return {"qp_top": qp_top,
            "kp": kp,
            "v": v,
            "Wv_words": Wv_words,
            "Wv_scales": Wv_scales,
            "bv": bv}


def reference(qp_top, kp, v, Wv_words, Wv_scales, bv):
    vp = (mxq(f64(v), 2, "e4m3") @ unpack_weight(Wv_words, Wv_scales, "e4m3")) + f64(bv)
    score = (mxq(f64(qp_top), 2, "e4m3") @ mxq(f64(kp), 2, "e4m3").transpose(0, 2, 1)) * (1.0 / np.sqrt(D))
    e = np.exp(score - score.max(0, keepdims=True))
    attn = e / e.sum(0, keepdims=True)
    return mxq(attn, 2, "e4m3") @ mxq(vp, 1, "e4m3")

@@ -1,0 +1,216 @@
+import math
+from contextlib import ExitStack
+
+import concourse.mybir as mybir
+from concourse.masks import make_identity
+
+BF16 = mybir.dt.bfloat16
+F32 = mybir.dt.float32
+I32 = mybir.dt.int32
+U8 = mybir.dt.uint8
+U32 = mybir.dt.uint32
+FP8X4 = mybir.dt.float8_e4m3fn_x4
+ADD = mybir.AluOpType.add
+SUBTRACT = mybir.AluOpType.subtract
+SIGMOID = mybir.ActivationFunctionType.Sigmoid
+
+B, L, D, DV, BN = 2, 512, 8192, 256, 64
+P = 128
+PACK = 4
+K_PASS = P * PACK
+PASSES = D // K_PASS
+WORDS_PASS = K_PASS // 2
+ROW_TILES = L // P
+
+HALVES = 2
+HALF_PASSES = PASSES // HALVES
+BANK_PASSES = 2
+HALF_BANKS = HALF_PASSES // BANK_PASSES
+HALF_WORDS = HALF_PASSES * P
+
+RAW_BUFS = 7
+AHEAD = RAW_BUFS - 1
+
+FLOPS = 2 * B * L * D * DV + 2 * B * BN * D * L + 2 * B * BN * L * DV
+
+
+def tile_bottleneck_attention_pa_k_kernel(tc, qp_top, kp, v, Wv_words, Wv_scales, bv, out):
+    nc = tc.nc
+    with ExitStack() as ctx:
+        ctx.enter_context(tc.manual_schedule())
+        keep = ctx.enter_context(tc.tile_pool(name="keep", bufs=1))
+        raw_pool = ctx.enter_context(tc.tile_pool(name="raw", bufs=RAW_BUFS))
+        grouped_pool = ctx.enter_context(tc.tile_pool(name="grouped", bufs=3))
+        code_pool = ctx.enter_context(tc.tile_pool(name="codes", bufs=3))
+        bank_pool = ctx.enter_context(tc.psum_pool(name="banks", bufs=6))
+        acc_pool = ctx.enter_context(tc.psum_pool(name="acc", bufs=2))
+
+        w_codes = keep.tile([P, PASSES, DV * PACK], U8, align_bytes=64)
+        w_planes = keep.tile([P, PASSES, DV], U8, align_bytes=64)
+        q_codes = keep.tile([P, PASSES * P], U32, align_bytes=64)
+        q_planes = keep.tile([P, PASSES * P], U8, align_bytes=64)
+        bias = keep.tile([P, DV], BF16)
+        ident = keep.tile([P, P], F32)
+        score0 = keep.tile([P, ROW_TILES, BN], F32)
+        diff = keep.tile([P, ROW_TILES, BN], F32)
+        vp_grouped = keep.tile([P, B, DV, PACK], BF16, align_bytes=64)
+        vp_codes = keep.tile([P, B * DV], U32, align_bytes=64)
+        vp_planes = keep.tile([P, B * DV], U8, align_bytes=64)
+        attn_grouped = keep.tile([P, B, BN, PACK], BF16, align_bytes=64)
+        attn_codes = keep.tile([P, B * BN], U32, align_bytes=64)
+        attn_planes = keep.tile([P, B * BN], U8, align_bytes=64)
+        result = keep.tile([P, DV], F32)
+        warm = keep.tile([P, 2], F32)
+
+        row_tiles = []
+        for b in range(B):
+            for t in range(ROW_TILES):
+                row_tiles.append(("v", b, t, v[b].rearrange("(p t) d -> t p d", t=ROW_TILES)[t]))
+        row_tiles.append(("q", 0, 0, qp_top.rearrange("b i d -> (b i) d")))
+        for b in range(B):
+            for t in range(ROW_TILES):
+                row_tiles.append(("kp", b, t, kp[b].rearrange("(p t) d -> t p d", t=ROW_TILES)[t]))
+        n_halves = HALVES * len(row_tiles)
+
+        raws = {}
+        groupeds = {}
+        codes = {}
+        accs = {}
+
+        def load(s):
+            if s < len(row_tiles):
+                raw = raw_pool.tile([P, D], BF16, name="raw")
+                nc.sync.dma_start(out=raw[:], in_=row_tiles[s][3])
+                raws[s] = raw
+
+        def transpose_half(j):
+            s, h = divmod(j, HALVES)
+            kind = row_tiles[s][0]
+            words = raws[s][:].bitcast(F32)
+            grouped = grouped_pool.tile([P, HALF_WORDS * PACK], BF16, align_bytes=64, name="grouped")
+            groupeds[j] = grouped
+            grouped_words = grouped[:].bitcast(F32)
+            for k in range(HALF_BANKS):
+                bank = bank_pool.tile([P, BANK_PASSES * 2, P], F32, name="bank")
+                for c in range(BANK_PASSES):
+                    first = (h * HALF_PASSES + k * BANK_PASSES + c) * WORDS_PASS
+                    for u in range(2):
+                        if kind == "v":
+                            cols = words[:, first + u : first + WORDS_PASS : 2]
+                        else:
+                            cols = words[:, first + u * P : first + (u + 1) * P]
+                        nc.tensor.transpose(bank[:, 2 * c + u, :], cols, ident[:])
+                src = bank[:].rearrange("p (c u) r -> p c r u", u=2)
+                dst = grouped_words[:, k * 2 * BANK_PASSES * P : (k + 1) * 2 * BANK_PASSES * P].rearrange(
+                    "p (c r u) -> p c r u", c=BANK_PASSES, u=2
+                )
+                if k == 0:
+                    nc.vector.tensor_copy(out=dst, in_=src)
+                else:
+                    nc.scalar.copy(out=dst, in_=src)
+
+        def quantise_half(j):
+            s, h = divmod(j, HALVES)
+            if row_tiles[s][0] == "q":
+                cols = slice(h * HALF_WORDS, (h + 1) * HALF_WORDS)
+                half_codes, half_planes = q_codes[:, cols], q_planes[:, cols]
+            else:
+                code_tile = code_pool.tile([P, HALF_WORDS], U32, align_bytes=64, name="code_tile")
+                plane_tile = code_pool.tile([P, HALF_WORDS], U8, align_bytes=64, name="plane_tile")
+                half_codes, half_planes = code_tile[:], plane_tile[:]
+            codes[j] = (half_codes, half_planes)
+            nc.vector.quantize_mx(out=half_codes.bitcast(FP8X4), scales=half_planes, in_=groupeds[j][:])
+
+        def multiply_half(j):
+            s, h = divmod(j, HALVES)
+            kind, b, t = row_tiles[s][0:3]
+            if kind == "q":
+                return
+            if h == 0:
+                accs[s] = acc_pool.tile([P, 512], F32, name="acc")
+            acc = accs[s]
+            half_codes, half_planes = codes[j]
+            for c in range(HALF_PASSES):
+                g = h * HALF_PASSES + c
+                rows = slice(c * P, (c + 1) * P)
+                if kind == "v":
+                    width = DV
+                    rhs, rhs_scale = w_codes[:, g, :], w_planes[:, g, :]
+                else:
+                    width = B * BN
+                    rhs, rhs_scale = q_codes[:, g * P : (g + 1) * P], q_planes[:, g * P : (g + 1) * P]
+                nc.tensor.matmul_mx(
+                    out=acc[:, 0:width],
+                    lhsT=half_codes[:, rows].bitcast(FP8X4),
+                    lhsT_scale=half_planes[:, rows],
+                    rhs=rhs.bitcast(FP8X4),
+                    rhs_scale=rhs_scale,
+                    start=(g == 0),
+                    stop=(g == PASSES - 1),
+                )
+            if h < HALVES - 1:
+                return
+            if kind == "v":
+                nc.vector.tensor_tensor(out=vp_grouped[:, b, :, t], in0=acc[:, 0:DV], in1=bias[:], op=ADD)
+            elif b == 0:
+                nc.scalar.copy(out=score0[:, t, :], in_=acc[:, 0:BN])
+            else:
+                nc.vector.tensor_tensor(out=diff[:, t, :], in0=acc[:, BN : 2 * BN], in1=score0[:, t, :], op=SUBTRACT)
+
+        nc.vector.memset(w_planes[:].rearrange("p g n -> p (g n)").bitcast(I32), 0)
+        nc.vector.memset(warm[:], 0.0)
+        nc.scalar.activation(out=warm[:, 1:2], in_=warm[:, 0:1], func=SIGMOID)
+        make_identity(nc, ident[:])
+        nc.scalar.dma_start(out=bias[:], in_=bv.partition_broadcast(P))
+        for quadrant in range(4):
+            nc.sync.dma_start(
+                out=w_planes[32 * quadrant : 32 * quadrant + 4, :, :].bitcast(I32),
+                in_=Wv_scales[:, 4 * quadrant : 4 * quadrant + 4, :].rearrange("g r n -> r g n").bitcast(I32),
+            )
+        load(0)
+        nc.sync.dma_start(
+            out=w_codes[:].bitcast(I32),
+            in_=Wv_words.rearrange("g p n t -> p g (n t)").bitcast(I32),
+        )
+        for s in range(1, AHEAD):
+            load(s)
+
+        for j in range(n_halves + 2):
+            if j % HALVES == 0:
+                load(j // HALVES + AHEAD)
+            if j < n_halves:
+                transpose_half(j)
+            if 1 <= j <= n_halves:
+                quantise_half(j - 1)
+            if j >= 2:
+                multiply_half(j - 2)
+            if j - 2 == HALVES * B * ROW_TILES - 1:
+                nc.vector.quantize_mx(
+                    out=vp_codes[:].bitcast(FP8X4),
+                    scales=vp_planes[:],
+                    in_=vp_grouped[:].rearrange("p b n t -> p (b n t)"),
+                )
+
+        scale = 1.0 / math.sqrt(D)
+        by_query = diff[:].rearrange("p t i -> p i t")
+        nc.scalar.activation(out=attn_grouped[:, 1, :, :], in_=by_query, func=SIGMOID, scale=scale)
+        nc.scalar.activation(out=attn_grouped[:, 0, :, :], in_=by_query, func=SIGMOID, scale=-scale)
+        nc.vector.quantize_mx(
+            out=attn_codes[:].bitcast(FP8X4),
+            scales=attn_planes[:],
+            in_=attn_grouped[:].rearrange("p b i t -> p (b i t)"),
+        )
+
+        final = acc_pool.tile([P, 512], F32, name="acc")
+        nc.tensor.matmul_mx(
+            out=final[:],
+            lhsT=attn_codes[:].bitcast(FP8X4),
+            lhsT_scale=attn_planes[:],
+            rhs=vp_codes[:].bitcast(FP8X4),
+            rhs_scale=vp_planes[:],
+            start=True,
+            stop=True,
+        )
+        nc.scalar.copy(out=result[0:BN, :], in_=final[0:BN, 0:DV])
+        nc.vector.tensor_copy(out=result[BN:P, :], in_=final[BN:P, DV : 2 * DV])
+        nc.sync.dma_start(out=out.rearrange("b i n -> (b i) n"), in_=result[:])

@@ -19,17 +19,19 @@ P = 128
 PACK = 4
 K_PASS = P * PACK
 PASSES = D // K_PASS
-WORDS_PASS = K_PASS // 2
 ROW_TILES = L // P
 
 HALVES = 2
 HALF_PASSES = PASSES // HALVES
+HALF_D = D // HALVES
+HALF_CODES = HALF_PASSES * P
 BANK_PASSES = 2
+BANK_F32 = 512
 HALF_BANKS = HALF_PASSES // BANK_PASSES
-HALF_WORDS = HALF_PASSES * P
 
-RAW_BUFS = 7
+RAW_BUFS = 10
 AHEAD = RAW_BUFS - 1
+SORT_AHEAD = 2
 
 FLOPS = 2 * B * L * D * DV + 2 * B * BN * D * L + 2 * B * BN * L * DV
 
@@ -40,17 +42,20 @@ def tile_bottleneck_attention_pa_k_kernel(tc, qp_top, kp, v, Wv_words, Wv_scales
         ctx.enter_context(tc.manual_schedule())
         keep = ctx.enter_context(tc.tile_pool(name="keep", bufs=1))
         raw_pool = ctx.enter_context(tc.tile_pool(name="raw", bufs=RAW_BUFS))
+        sorted_pool = ctx.enter_context(tc.tile_pool(name="sorted", bufs=3))
         grouped_pool = ctx.enter_context(tc.tile_pool(name="grouped", bufs=3))
         code_pool = ctx.enter_context(tc.tile_pool(name="codes", bufs=3))
         bank_pool = ctx.enter_context(tc.psum_pool(name="banks", bufs=6))
-        acc_pool = ctx.enter_context(tc.psum_pool(name="acc", bufs=2))
+        acc_pool = ctx.enter_context(tc.psum_pool(name="acc", bufs=1))
 
         w_codes = keep.tile([P, PASSES, DV * PACK], U8, align_bytes=64)
         w_planes = keep.tile([P, PASSES, DV], U8, align_bytes=64)
         q_codes = keep.tile([P, PASSES * P], U32, align_bytes=64)
         q_planes = keep.tile([P, PASSES * P], U8, align_bytes=64)
-        bias = keep.tile([P, DV], BF16)
         ident = keep.tile([P, P], F32)
+        ones = keep.tile([P, P], BF16)
+        bias_row = keep.tile([P, DV], BF16)
+        bias = keep.tile([P, DV], F32)
         score0 = keep.tile([P, ROW_TILES, BN], F32)
         diff = keep.tile([P, ROW_TILES, BN], F32)
         vp_grouped = keep.tile([P, B, DV, PACK], BF16, align_bytes=64)
@@ -62,73 +67,98 @@ def tile_bottleneck_attention_pa_k_kernel(tc, qp_top, kp, v, Wv_words, Wv_scales
         result = keep.tile([P, DV], F32)
         warm = keep.tile([P, 2], F32)
 
-        row_tiles = []
+        halves = [("q", 0, 0, h) for h in range(HALVES)]
         for b in range(B):
             for t in range(ROW_TILES):
-                row_tiles.append(("v", b, t, v[b].rearrange("(p t) d -> t p d", t=ROW_TILES)[t]))
-        row_tiles.append(("q", 0, 0, qp_top.rearrange("b i d -> (b i) d")))
-        for b in range(B):
-            for t in range(ROW_TILES):
-                row_tiles.append(("kp", b, t, kp[b].rearrange("(p t) d -> t p d", t=ROW_TILES)[t]))
-        n_halves = HALVES * len(row_tiles)
+                for h in range(HALVES):
+                    halves.append(("v", b, t, h))
+                    halves.append(("kp", b, t, h))
+        n_halves = len(halves)
 
-        raws = {}
+        words = {}
         groupeds = {}
         codes = {}
         accs = {}
 
-        def load(s):
-            if s < len(row_tiles):
-                raw = raw_pool.tile([P, D], BF16, name="raw")
-                nc.sync.dma_start(out=raw[:], in_=row_tiles[s][3])
-                raws[s] = raw
+        def load(j):
+            if j >= n_halves:
+                return
+            kind, b, t, h = halves[j]
+            if kind == "q":
+                rows = qp_top.rearrange("b i d -> (b i) d")
+            elif kind == "v":
+                rows = v[b].rearrange("(p t) d -> t p d", t=ROW_TILES)[t]
+            else:
+                rows = kp[b].rearrange("(p t) d -> t p d", t=ROW_TILES)[t]
+            raw = raw_pool.tile([P, HALF_D], BF16, name="raw")
+            nc.sync.dma_start(out=raw[:], in_=rows[:, h * HALF_D : (h + 1) * HALF_D])
+            words[j] = raw[:].bitcast(F32)
+
+        def load_weight_scales():
+            for quadrant in range(4):
+                nc.sync.dma_start(
+                    out=w_planes[32 * quadrant : 32 * quadrant + 4, :, :].bitcast(I32),
+                    in_=Wv_scales[:, 4 * quadrant : 4 * quadrant + 4, :].rearrange("g r n -> r g n").bitcast(I32),
+                )
+
+        def load_weight_half(h):
+            g = slice(h * HALF_PASSES, (h + 1) * HALF_PASSES)
+            nc.sync.dma_start(
+                out=w_codes[:, g, :].bitcast(I32),
+                in_=Wv_words[g].rearrange("g p n t -> p g (n t)").bitcast(I32),
+            )
+
+        def sort_half(j):
+            if j >= n_halves or halves[j][0] != "v":
+                return
+            sorted_words = sorted_pool.tile([P, HALF_D // 2], F32, name="sorted_words")
+            nc.vector.tensor_copy(
+                out=sorted_words[:].rearrange("p (c u w) -> p c u w", u=2, w=P),
+                in_=words[j].rearrange("p (c w u) -> p c u w", u=2, w=P),
+            )
+            words[j] = sorted_words[:]
 
         def transpose_half(j):
-            s, h = divmod(j, HALVES)
-            kind = row_tiles[s][0]
-            words = raws[s][:].bitcast(F32)
-            grouped = grouped_pool.tile([P, HALF_WORDS * PACK], BF16, align_bytes=64, name="grouped")
+            kind = halves[j][0]
+            grouped = grouped_pool.tile([P, HALF_CODES * PACK], BF16, align_bytes=64, name="grouped")
             groupeds[j] = grouped
             grouped_words = grouped[:].bitcast(F32)
             for k in range(HALF_BANKS):
                 bank = bank_pool.tile([P, BANK_PASSES * 2, P], F32, name="bank")
-                for c in range(BANK_PASSES):
-                    first = (h * HALF_PASSES + k * BANK_PASSES + c) * WORDS_PASS
-                    for u in range(2):
-                        if kind == "v":
-                            cols = words[:, first + u : first + WORDS_PASS : 2]
-                        else:
-                            cols = words[:, first + u * P : first + (u + 1) * P]
-                        nc.tensor.transpose(bank[:, 2 * c + u, :], cols, ident[:])
+                for i in range(BANK_PASSES * 2):
+                    first = (k * BANK_PASSES * 2 + i) * P
+                    nc.tensor.transpose(bank[:, i, :], words[j][:, first : first + P], ident[:])
                 src = bank[:].rearrange("p (c u) r -> p c r u", u=2)
-                dst = grouped_words[:, k * 2 * BANK_PASSES * P : (k + 1) * 2 * BANK_PASSES * P].rearrange(
+                dst = grouped_words[:, k * BANK_F32 : (k + 1) * BANK_F32].rearrange(
                     "p (c r u) -> p c r u", c=BANK_PASSES, u=2
                 )
-                if k == 0:
+                if kind == "kp" and k == 0:
                     nc.vector.tensor_copy(out=dst, in_=src)
                 else:
                     nc.scalar.copy(out=dst, in_=src)
 
         def quantise_half(j):
-            s, h = divmod(j, HALVES)
-            if row_tiles[s][0] == "q":
-                cols = slice(h * HALF_WORDS, (h + 1) * HALF_WORDS)
+            kind, b, t, h = halves[j]
+            if kind == "q":
+                cols = slice(h * HALF_CODES, (h + 1) * HALF_CODES)
                 half_codes, half_planes = q_codes[:, cols], q_planes[:, cols]
             else:
-                code_tile = code_pool.tile([P, HALF_WORDS], U32, align_bytes=64, name="code_tile")
-                plane_tile = code_pool.tile([P, HALF_WORDS], U8, align_bytes=64, name="plane_tile")
+                code_tile = code_pool.tile([P, HALF_CODES], U32, align_bytes=64, name="code_tile")
+                plane_tile = code_pool.tile([P, HALF_CODES], U8, align_bytes=64, name="plane_tile")
                 half_codes, half_planes = code_tile[:], plane_tile[:]
             codes[j] = (half_codes, half_planes)
             nc.vector.quantize_mx(out=half_codes.bitcast(FP8X4), scales=half_planes, in_=groupeds[j][:])
 
         def multiply_half(j):
-            s, h = divmod(j, HALVES)
-            kind, b, t = row_tiles[s][0:3]
+            kind, b, t, h = halves[j]
             if kind == "q":
                 return
             if h == 0:
-                accs[s] = acc_pool.tile([P, 512], F32, name="acc")
-            acc = accs[s]
+                if kind == "v":
+                    accs[kind] = acc_pool.tile([P, BANK_F32], F32, name="acc_v")
+                else:
+                    accs[kind] = acc_pool.tile([P, BANK_F32], F32, name="acc_kp")
+            acc = accs[kind]
             half_codes, half_planes = codes[j]
             for c in range(HALF_PASSES):
                 g = h * HALF_PASSES + c
@@ -156,40 +186,42 @@ def tile_bottleneck_attention_pa_k_kernel(tc, qp_top, kp, v, Wv_words, Wv_scales
                 nc.scalar.copy(out=score0[:, t, :], in_=acc[:, 0:BN])
             else:
                 nc.vector.tensor_tensor(out=diff[:, t, :], in0=acc[:, BN : 2 * BN], in1=score0[:, t, :], op=SUBTRACT)
+            if kind == "kp" and t == ROW_TILES - 1:
+                nc.vector.quantize_mx(
+                    out=vp_codes[:, b * DV : (b + 1) * DV].bitcast(FP8X4),
+                    scales=vp_planes[:, b * DV : (b + 1) * DV],
+                    in_=vp_grouped[:, b, :, :].rearrange("p n t -> p (n t)"),
+                )
 
         nc.vector.memset(w_planes[:].rearrange("p g n -> p (g n)").bitcast(I32), 0)
         nc.vector.memset(warm[:], 0.0)
         nc.scalar.activation(out=warm[:, 1:2], in_=warm[:, 0:1], func=SIGMOID)
         make_identity(nc, ident[:])
-        nc.scalar.dma_start(out=bias[:], in_=bv.partition_broadcast(P))
-        for quadrant in range(4):
-            nc.sync.dma_start(
-                out=w_planes[32 * quadrant : 32 * quadrant + 4, :, :].bitcast(I32),
-                in_=Wv_scales[:, 4 * quadrant : 4 * quadrant + 4, :].rearrange("g r n -> r g n").bitcast(I32),
-            )
-        load(0)
-        nc.sync.dma_start(
-            out=w_codes[:].bitcast(I32),
-            in_=Wv_words.rearrange("g p n t -> p g (n t)").bitcast(I32),
-        )
-        for s in range(1, AHEAD):
-            load(s)
+        nc.gpsimd.memset(ones[:], 1.0)
+        nc.gpsimd.memset(bias_row[:], 0.0)
+        nc.scalar.dma_start(out=bias_row[0:1, :], in_=bv.rearrange("(o n) -> o n", o=1))
+
+        for j in range(AHEAD):
+            load(j)
+            kind, b, t, h = halves[j]
+            if kind == "v" and (b, t) == (0, 0):
+                if h == 0:
+                    load_weight_scales()
+                load_weight_half(h)
+
+        spread = acc_pool.tile([P, BANK_F32], F32, name="acc_v")
+        nc.tensor.matmul(out=spread[:, 0:DV], lhsT=ones[:], rhs=bias_row[:], start=True, stop=True)
+        nc.scalar.copy(out=bias[:], in_=spread[:, 0:DV])
 
         for j in range(n_halves + 2):
-            if j % HALVES == 0:
-                load(j // HALVES + AHEAD)
+            load(j + AHEAD)
             if j < n_halves:
                 transpose_half(j)
             if 1 <= j <= n_halves:
                 quantise_half(j - 1)
             if j >= 2:
                 multiply_half(j - 2)
-            if j - 2 == HALVES * B * ROW_TILES - 1:
-                nc.vector.quantize_mx(
-                    out=vp_codes[:].bitcast(FP8X4),
-                    scales=vp_planes[:],
-                    in_=vp_grouped[:].rearrange("p b n t -> p (b n t)"),
-                )
+            sort_half(j + SORT_AHEAD)
 
         scale = 1.0 / math.sqrt(D)
         by_query = diff[:].rearrange("p t i -> p i t")
@@ -201,7 +233,7 @@ def tile_bottleneck_attention_pa_k_kernel(tc, qp_top, kp, v, Wv_words, Wv_scales
             in_=attn_grouped[:].rearrange("p b i t -> p (b i t)"),
         )
 
-        final = acc_pool.tile([P, 512], F32, name="acc")
+        final = acc_pool.tile([P, BANK_F32], F32, name="acc_v")
         nc.tensor.matmul_mx(
             out=final[:],
             lhsT=attn_codes[:].bitcast(FP8X4),

@@ -30,8 +30,7 @@ BANK_F32 = 512
 HALF_BANKS = HALF_PASSES // BANK_PASSES
 
 RAW_BUFS = 10
-AHEAD = RAW_BUFS - 1
-SORT_AHEAD = 2
+AHEAD = RAW_BUFS - 2
 
 FLOPS = 2 * B * L * D * DV + 2 * B * BN * D * L + 2 * B * BN * L * DV
 
@@ -42,9 +41,9 @@ def tile_bottleneck_attention_pa_k_kernel(tc, qp_top, kp, v, Wv_words, Wv_scales
         ctx.enter_context(tc.manual_schedule())
         keep = ctx.enter_context(tc.tile_pool(name="keep", bufs=1))
         raw_pool = ctx.enter_context(tc.tile_pool(name="raw", bufs=RAW_BUFS))
-        sorted_pool = ctx.enter_context(tc.tile_pool(name="sorted", bufs=3))
+        sorted_pool = ctx.enter_context(tc.tile_pool(name="sorted", bufs=2))
         grouped_pool = ctx.enter_context(tc.tile_pool(name="grouped", bufs=3))
-        code_pool = ctx.enter_context(tc.tile_pool(name="codes", bufs=3))
+        code_pool = ctx.enter_context(tc.tile_pool(name="codes", bufs=4))
         bank_pool = ctx.enter_context(tc.psum_pool(name="banks", bufs=6))
         acc_pool = ctx.enter_context(tc.psum_pool(name="acc", bufs=1))
 
@@ -119,7 +118,6 @@ def tile_bottleneck_attention_pa_k_kernel(tc, qp_top, kp, v, Wv_words, Wv_scales
             words[j] = sorted_words[:]
 
         def transpose_half(j):
-            kind = halves[j][0]
             grouped = grouped_pool.tile([P, HALF_CODES * PACK], BF16, align_bytes=64, name="grouped")
             groupeds[j] = grouped
             grouped_words = grouped[:].bitcast(F32)
@@ -132,10 +130,7 @@ def tile_bottleneck_attention_pa_k_kernel(tc, qp_top, kp, v, Wv_words, Wv_scales
                 dst = grouped_words[:, k * BANK_F32 : (k + 1) * BANK_F32].rearrange(
                     "p (c r u) -> p c r u", c=BANK_PASSES, u=2
                 )
-                if kind == "kp" and k == 0:
-                    nc.vector.tensor_copy(out=dst, in_=src)
-                else:
-                    nc.scalar.copy(out=dst, in_=src)
+                nc.scalar.copy(out=dst, in_=src)
 
         def quantise_half(j):
             kind, b, t, h = halves[j]
@@ -209,19 +204,28 @@ def tile_bottleneck_attention_pa_k_kernel(tc, qp_top, kp, v, Wv_words, Wv_scales
                     load_weight_scales()
                 load_weight_half(h)
 
-        spread = acc_pool.tile([P, BANK_F32], F32, name="acc_v")
-        nc.tensor.matmul(out=spread[:, 0:DV], lhsT=ones[:], rhs=bias_row[:], start=True, stop=True)
-        nc.scalar.copy(out=bias[:], in_=spread[:, 0:DV])
+        def spread_bias():
+            spread = acc_pool.tile([P, BANK_F32], F32, name="acc_v")
+            nc.tensor.matmul(out=spread[:, 0:DV], lhsT=ones[:], rhs=bias_row[:], start=True, stop=True)
+            nc.scalar.copy(out=bias[:], in_=spread[:, 0:DV])
 
-        for j in range(n_halves + 2):
-            load(j + AHEAD)
-            if j < n_halves:
-                transpose_half(j)
-            if 1 <= j <= n_halves:
-                quantise_half(j - 1)
-            if j >= 2:
-                multiply_half(j - 2)
-            sort_half(j + SORT_AHEAD)
+        n_pairs = n_halves // 2
+        for s in range(n_pairs + 1):
+            first, second = 2 * s, 2 * s + 1
+            load(first + AHEAD)
+            load(second + AHEAD)
+            if s >= 1:
+                quantise_half(second - 2)
+            sort_half(first + 2)
+            if s < n_pairs:
+                transpose_half(first)
+                transpose_half(second)
+                quantise_half(first)
+            if s == 0:
+                spread_bias()
+            if s >= 1:
+                multiply_half(first - 2)
+                multiply_half(second - 2)
 
         scale = 1.0 / math.sqrt(D)
         by_query = diff[:].rearrange("p t i -> p i t")

@@ -21,16 +21,18 @@ K_PASS = P * PACK
 PASSES = D // K_PASS
 ROW_TILES = L // P
 
-HALVES = 2
-HALF_PASSES = PASSES // HALVES
-HALF_D = D // HALVES
-HALF_CODES = HALF_PASSES * P
+LONG, SHORT = 8, 4
+SHORT_TILES = 3
+V_TILES_FIRST = 5
+UNSORTED_TILES = 0
 BANK_PASSES = 2
 BANK_F32 = 512
-HALF_BANKS = HALF_PASSES // BANK_PASSES
 
 RAW_BUFS = 10
-AHEAD = RAW_BUFS - 2
+LOAD_AHEAD = RAW_BUFS - 1
+SORT_AHEAD = 2
+QUANTISE_BEHIND = 2
+MULTIPLY_BEHIND = 3
 
 FLOPS = 2 * B * L * D * DV + 2 * B * BN * D * L + 2 * B * BN * L * DV
 
@@ -41,14 +43,14 @@ def tile_bottleneck_attention_pa_k_kernel(tc, qp_top, kp, v, Wv_words, Wv_scales
         ctx.enter_context(tc.manual_schedule())
         keep = ctx.enter_context(tc.tile_pool(name="keep", bufs=1))
         raw_pool = ctx.enter_context(tc.tile_pool(name="raw", bufs=RAW_BUFS))
-        sorted_pool = ctx.enter_context(tc.tile_pool(name="sorted", bufs=2))
-        grouped_pool = ctx.enter_context(tc.tile_pool(name="grouped", bufs=3))
-        code_pool = ctx.enter_context(tc.tile_pool(name="codes", bufs=4))
+        sorted_pool = ctx.enter_context(tc.tile_pool(name="sorted", bufs=4))
+        grouped_pool = ctx.enter_context(tc.tile_pool(name="grouped", bufs=4))
+        code_pool = ctx.enter_context(tc.tile_pool(name="codes", bufs=6))
         bank_pool = ctx.enter_context(tc.psum_pool(name="banks", bufs=6))
         acc_pool = ctx.enter_context(tc.psum_pool(name="acc", bufs=1))
 
         w_codes = keep.tile([P, PASSES, DV * PACK], U8, align_bytes=64)
-        w_planes = keep.tile([P, PASSES, DV], U8, align_bytes=64)
+        w_planes = keep.tile([P, PASSES // SHORT, DV], U8, align_bytes=64)
         q_codes = keep.tile([P, PASSES * P], U32, align_bytes=64)
         q_planes = keep.tile([P, PASSES * P], U8, align_bytes=64)
         ident = keep.tile([P, P], F32)
@@ -66,127 +68,166 @@ def tile_bottleneck_attention_pa_k_kernel(tc, qp_top, kp, v, Wv_words, Wv_scales
         result = keep.tile([P, DV], F32)
         warm = keep.tile([P, 2], F32)
 
-        halves = [("q", 0, 0, h) for h in range(HALVES)]
-        for b in range(B):
-            for t in range(ROW_TILES):
-                for h in range(HALVES):
-                    halves.append(("v", b, t, h))
-                    halves.append(("kp", b, t, h))
-        n_halves = len(halves)
+        def cut(kind, tile, size):
+            return [(kind, tile // ROW_TILES, tile % ROW_TILES, g, size) for g in range(0, PASSES, size)]
+
+        pieces = []
+        for tile in range(V_TILES_FIRST):
+            pieces += cut("v", tile, SHORT if tile < SHORT_TILES else LONG)
+        pieces += cut("q", 0, LONG)
+        rest = [piece for tile in range(V_TILES_FIRST, B * ROW_TILES) for piece in cut("v", tile, LONG)]
+        keys = [piece for tile in range(B * ROW_TILES) for piece in cut("kp", tile, LONG)]
+        keys = keys[:-1] + cut("kp", B * ROW_TILES - 1, SHORT)[2:]
+        for j, piece in enumerate(keys):
+            pieces += rest[j : j + 1] + [piece]
+        n_pieces = len(pieces)
 
         words = {}
         groupeds = {}
         codes = {}
         accs = {}
 
-        def load(j):
-            if j >= n_halves:
+        def load_weight(a):
+            g = slice(SHORT * a, SHORT * (a + 1))
+            for quadrant in range(4):
+                nc.sync.dma_start(
+                    out=w_planes[32 * quadrant : 32 * quadrant + 16, a, :].bitcast(I32),
+                    in_=Wv_scales[g, 4 * quadrant : 4 * quadrant + 4, :].bitcast(I32),
+                )
+            nc.sync.dma_start(
+                out=w_codes[:, g, :].bitcast(I32),
+                in_=Wv_words[g].rearrange("g p n t -> p g (n t)").bitcast(I32),
+            )
+
+        def load(i):
+            if i >= n_pieces:
                 return
-            kind, b, t, h = halves[j]
+            kind, b, t, g, size = pieces[i]
             if kind == "q":
                 rows = qp_top.rearrange("b i d -> (b i) d")
             elif kind == "v":
                 rows = v[b].rearrange("(p t) d -> t p d", t=ROW_TILES)[t]
             else:
                 rows = kp[b].rearrange("(p t) d -> t p d", t=ROW_TILES)[t]
-            raw = raw_pool.tile([P, HALF_D], BF16, name="raw")
-            nc.sync.dma_start(out=raw[:], in_=rows[:, h * HALF_D : (h + 1) * HALF_D])
-            words[j] = raw[:].bitcast(F32)
+            raw = raw_pool.tile([P, size * K_PASS], BF16, name="raw")
+            nc.sync.dma_start(out=raw[:], in_=rows[:, g * K_PASS : (g + size) * K_PASS])
+            words[i] = raw[:].bitcast(F32)
+            if (kind, b, t) == ("v", 0, 0):
+                load_weight(g // SHORT)
 
-        def load_weight_scales():
-            for quadrant in range(4):
-                nc.sync.dma_start(
-                    out=w_planes[32 * quadrant : 32 * quadrant + 4, :, :].bitcast(I32),
-                    in_=Wv_scales[:, 4 * quadrant : 4 * quadrant + 4, :].rearrange("g r n -> r g n").bitcast(I32),
-                )
-
-        def load_weight_half(h):
-            g = slice(h * HALF_PASSES, (h + 1) * HALF_PASSES)
-            nc.sync.dma_start(
-                out=w_codes[:, g, :].bitcast(I32),
-                in_=Wv_words[g].rearrange("g p n t -> p g (n t)").bitcast(I32),
-            )
-
-        def sort_half(j):
-            if j >= n_halves or halves[j][0] != "v":
+        def sort_piece(i):
+            if i >= n_pieces or pieces[i][0] != "v" or pieces[i][1] * ROW_TILES + pieces[i][2] < UNSORTED_TILES:
                 return
-            sorted_words = sorted_pool.tile([P, HALF_D // 2], F32, name="sorted_words")
+            size = pieces[i][4]
+            sorted_words = sorted_pool.tile([P, size * K_PASS // 2], F32, name="sorted_words")
             nc.vector.tensor_copy(
                 out=sorted_words[:].rearrange("p (c u w) -> p c u w", u=2, w=P),
-                in_=words[j].rearrange("p (c w u) -> p c u w", u=2, w=P),
+                in_=words[i].rearrange("p (c w u) -> p c u w", u=2, w=P),
             )
-            words[j] = sorted_words[:]
+            words[i] = sorted_words[:]
 
-        def transpose_half(j):
-            grouped = grouped_pool.tile([P, HALF_CODES * PACK], BF16, align_bytes=64, name="grouped")
-            groupeds[j] = grouped
+        def transpose_piece(i):
+            kind, b, t, g, size = pieces[i]
+            grouped = grouped_pool.tile([P, size * K_PASS], BF16, align_bytes=64, name="grouped")
+            groupeds[i] = grouped
             grouped_words = grouped[:].bitcast(F32)
-            for k in range(HALF_BANKS):
+            left = []
+            for k in range(size // BANK_PASSES):
                 bank = bank_pool.tile([P, BANK_PASSES * 2, P], F32, name="bank")
-                for i in range(BANK_PASSES * 2):
-                    first = (k * BANK_PASSES * 2 + i) * P
-                    nc.tensor.transpose(bank[:, i, :], words[j][:, first : first + P], ident[:])
+                for j in range(BANK_PASSES * 2):
+                    first = (k * BANK_PASSES * 2 + j) * P
+                    block = words[i][:, first : first + P]
+                    if kind == "v" and b * ROW_TILES + t < UNSORTED_TILES:
+                        first = (k * BANK_PASSES + j // 2) * 2 * P
+                        block = words[i][:, first + j % 2 : first + 2 * P : 2]
+                    nc.tensor.transpose(bank[:, j, :], block, ident[:])
                 src = bank[:].rearrange("p (c u) r -> p c r u", u=2)
                 dst = grouped_words[:, k * BANK_F32 : (k + 1) * BANK_F32].rearrange(
                     "p (c r u) -> p c r u", c=BANK_PASSES, u=2
                 )
-                nc.scalar.copy(out=dst, in_=src)
+                if kind == "kp" and k == 2:
+                    left.append((dst, src))
+                else:
+                    nc.scalar.copy(out=dst, in_=src)
+            return left
 
-        def quantise_half(j):
-            kind, b, t, h = halves[j]
+        def quantise_piece(i):
+            kind, b, t, g, size = pieces[i]
             if kind == "q":
-                cols = slice(h * HALF_CODES, (h + 1) * HALF_CODES)
-                half_codes, half_planes = q_codes[:, cols], q_planes[:, cols]
+                cols = slice(g * P, (g + size) * P)
+                piece_codes, piece_planes = q_codes[:, cols], q_planes[:, cols]
             else:
-                code_tile = code_pool.tile([P, HALF_CODES], U32, align_bytes=64, name="code_tile")
-                plane_tile = code_pool.tile([P, HALF_CODES], U8, align_bytes=64, name="plane_tile")
-                half_codes, half_planes = code_tile[:], plane_tile[:]
-            codes[j] = (half_codes, half_planes)
-            nc.vector.quantize_mx(out=half_codes.bitcast(FP8X4), scales=half_planes, in_=groupeds[j][:])
+                code_tile = code_pool.tile([P, size * P], U32, align_bytes=64, name="code_tile")
+                plane_tile = code_pool.tile([P, size * P], U8, align_bytes=64, name="plane_tile")
+                piece_codes, piece_planes = code_tile[:], plane_tile[:]
+            codes[i] = (piece_codes, piece_planes)
+            nc.vector.quantize_mx(out=piece_codes.bitcast(FP8X4), scales=piece_planes, in_=groupeds[i][:])
 
-        def multiply_half(j):
-            kind, b, t, h = halves[j]
+        def multiply_piece(i):
+            kind, b, t, g, size = pieces[i]
             if kind == "q":
                 return
-            if h == 0:
-                if kind == "v":
-                    accs[kind] = acc_pool.tile([P, BANK_F32], F32, name="acc_v")
+            if kind == "kp" and g == 0:
+                if b * ROW_TILES + t >= B * ROW_TILES - V_TILES_FIRST and t % 2 == 1:
+                    acc_v = acc_pool.tile([P, BANK_F32], F32, name="acc_v")
+                    accs[kind, b, t] = acc_v
                 else:
-                    accs[kind] = acc_pool.tile([P, BANK_F32], F32, name="acc_kp")
-            acc = accs[kind]
-            half_codes, half_planes = codes[j]
-            for c in range(HALF_PASSES):
-                g = h * HALF_PASSES + c
+                    acc_kp = acc_pool.tile([P, BANK_F32], F32, name="acc_kp")
+                    accs[kind, b, t] = acc_kp
+            if kind == "v" and g == 0:
+                if t % 2 == 1:
+                    accs[kind, b, t] = accs[kind, b, t - 1]
+                elif (b * ROW_TILES + t) % 4 == 2 and b * ROW_TILES + t < V_TILES_FIRST:
+                    acc_kp = acc_pool.tile([P, BANK_F32], F32, name="acc_kp")
+                    accs[kind, b, t] = acc_kp
+                else:
+                    acc_v = acc_pool.tile([P, BANK_F32], F32, name="acc_v")
+                    accs[kind, b, t] = acc_v
+            acc = accs[kind, b, t]
+            left_col = t % 2 * DV if kind == "v" else 0
+            piece_codes, piece_planes = codes[i]
+            for c in range(size):
                 rows = slice(c * P, (c + 1) * P)
                 if kind == "v":
                     width = DV
-                    rhs, rhs_scale = w_codes[:, g, :], w_planes[:, g, :]
+                    rhs, rhs_scale = w_codes[:, g + c, :], w_planes[4 * ((g + c) % SHORT) : P, (g + c) // SHORT, :]
                 else:
                     width = B * BN
-                    rhs, rhs_scale = q_codes[:, g * P : (g + 1) * P], q_planes[:, g * P : (g + 1) * P]
+                    cols = slice((g + c) * P, (g + c + 1) * P)
+                    rhs, rhs_scale = q_codes[:, cols], q_planes[:, cols]
                 nc.tensor.matmul_mx(
-                    out=acc[:, 0:width],
-                    lhsT=half_codes[:, rows].bitcast(FP8X4),
-                    lhsT_scale=half_planes[:, rows],
+                    out=acc[:, left_col : left_col + width],
+                    lhsT=piece_codes[:, rows].bitcast(FP8X4),
+                    lhsT_scale=piece_planes[:, rows],
                     rhs=rhs.bitcast(FP8X4),
                     rhs_scale=rhs_scale,
-                    start=(g == 0),
-                    stop=(g == PASSES - 1),
+                    start=(g + c == 0),
+                    stop=(g + c == PASSES - 1),
                 )
-            if h < HALVES - 1:
+
+        def finish_row_tile(i):
+            kind, b, t, g, size = pieces[i]
+            if kind == "q" or g + size < PASSES:
                 return
+            acc = accs[kind, b, t]
             if kind == "v":
-                nc.vector.tensor_tensor(out=vp_grouped[:, b, :, t], in0=acc[:, 0:DV], in1=bias[:], op=ADD)
+                if t % 2 == 1:
+                    nc.vector.tensor_tensor(
+                        out=vp_grouped[:, b, :, t - 1 : t + 1],
+                        in0=acc[:].rearrange("p (j n) -> p n j", j=2),
+                        in1=bias[:].unsqueeze(2).to_broadcast([P, DV, 2]),
+                        op=ADD,
+                    )
+                if t == ROW_TILES - 1:
+                    nc.vector.quantize_mx(
+                        out=vp_codes[:, b * DV : (b + 1) * DV].bitcast(FP8X4),
+                        scales=vp_planes[:, b * DV : (b + 1) * DV],
+                        in_=vp_grouped[:, b, :, :].rearrange("p n t -> p (n t)"),
+                    )
             elif b == 0:
                 nc.scalar.copy(out=score0[:, t, :], in_=acc[:, 0:BN])
             else:
                 nc.vector.tensor_tensor(out=diff[:, t, :], in0=acc[:, BN : 2 * BN], in1=score0[:, t, :], op=SUBTRACT)
-            if kind == "kp" and t == ROW_TILES - 1:
-                nc.vector.quantize_mx(
-                    out=vp_codes[:, b * DV : (b + 1) * DV].bitcast(FP8X4),
-                    scales=vp_planes[:, b * DV : (b + 1) * DV],
-                    in_=vp_grouped[:, b, :, :].rearrange("p n t -> p (n t)"),
-                )
 
         nc.vector.memset(w_planes[:].rearrange("p g n -> p (g n)").bitcast(I32), 0)
         nc.vector.memset(warm[:], 0.0)
@@ -196,36 +237,45 @@ def tile_bottleneck_attention_pa_k_kernel(tc, qp_top, kp, v, Wv_words, Wv_scales
         nc.gpsimd.memset(bias_row[:], 0.0)
         nc.scalar.dma_start(out=bias_row[0:1, :], in_=bv.rearrange("(o n) -> o n", o=1))
 
-        for j in range(AHEAD):
-            load(j)
-            kind, b, t, h = halves[j]
-            if kind == "v" and (b, t) == (0, 0):
-                if h == 0:
-                    load_weight_scales()
-                load_weight_half(h)
-
         def spread_bias():
-            spread = acc_pool.tile([P, BANK_F32], F32, name="acc_v")
+            spread = acc_pool.tile([P, BANK_F32], F32, name="acc_kp")
             nc.tensor.matmul(out=spread[:, 0:DV], lhsT=ones[:], rhs=bias_row[:], start=True, stop=True)
             nc.scalar.copy(out=bias[:], in_=spread[:, 0:DV])
 
-        n_pairs = n_halves // 2
-        for s in range(n_pairs + 1):
-            first, second = 2 * s, 2 * s + 1
-            load(first + AHEAD)
-            load(second + AHEAD)
-            if s >= 1:
-                quantise_half(second - 2)
-            sort_half(first + 2)
-            if s < n_pairs:
-                transpose_half(first)
-                transpose_half(second)
-                quantise_half(first)
-            if s == 0:
+        for i in range(LOAD_AHEAD):
+            load(i)
+        for i in range(SORT_AHEAD):
+            sort_piece(i)
+        short_pieces = len([piece for piece in pieces[:4] if piece[4] == SHORT])
+        quantised = 0
+        multiplied = 0
+        closed = []
+        for i in range(n_pieces):
+            load(i + LOAD_AHEAD)
+            left = transpose_piece(i)
+            while quantised <= i - QUANTISE_BEHIND:
+                quantise_piece(quantised)
+                quantised += 1
+            for j in closed:
+                finish_row_tile(j)
+            closed = []
+            for dst, src in left:
+                nc.vector.tensor_copy(out=dst, in_=src)
+            sort_piece(i + SORT_AHEAD)
+            if i == 0:
                 spread_bias()
-            if s >= 1:
-                multiply_half(first - 2)
-                multiply_half(second - 2)
+            if i < short_pieces or i >= n_pieces - 2 or (i - short_pieces) % 2 == 1:
+                while multiplied <= i - MULTIPLY_BEHIND:
+                    multiply_piece(multiplied)
+                    closed.append(multiplied)
+                    multiplied += 1
+        for i in range(quantised, n_pieces):
+            quantise_piece(i)
+        for j in closed:
+            finish_row_tile(j)
+        for i in range(multiplied, n_pieces):
+            multiply_piece(i)
+            finish_row_tile(i)
 
         scale = 1.0 / math.sqrt(D)
         by_query = diff[:].rearrange("p t i -> p i t")

@@ -23,8 +23,8 @@ ROW_TILES = L // P
 
 LONG, SHORT = 8, 4
 SHORT_TILES = 3
-V_TILES_FIRST = 5
-UNSORTED_TILES = 0
+V_TILES_FIRST = 6
+UNSORTED_TILES = 1
 BANK_PASSES = 2
 BANK_F32 = 512
 
@@ -168,7 +168,7 @@ def tile_bottleneck_attention_pa_k_kernel(tc, qp_top, kp, v, Wv_words, Wv_scales
             if kind == "q":
                 return
             if kind == "kp" and g == 0:
-                if b * ROW_TILES + t >= B * ROW_TILES - V_TILES_FIRST and t % 2 == 1:
+                if b * ROW_TILES + t >= B * ROW_TILES - V_TILES_FIRST and (t - V_TILES_FIRST) % 2 == 0:
                     acc_v = acc_pool.tile([P, BANK_F32], F32, name="acc_v")
                     accs[kind, b, t] = acc_v
                 else:
@@ -229,6 +229,12 @@ def tile_bottleneck_attention_pa_k_kernel(tc, qp_top, kp, v, Wv_words, Wv_scales
             else:
                 nc.vector.tensor_tensor(out=diff[:, t, :], in0=acc[:, BN : 2 * BN], in1=score0[:, t, :], op=SUBTRACT)
 
+        def softmax(tiles):
+            scale = 1.0 / math.sqrt(D)
+            by_query = diff[:, tiles, :].rearrange("p t i -> p i t")
+            nc.scalar.activation(out=attn_grouped[:, 1, :, tiles], in_=by_query, func=SIGMOID, scale=scale)
+            nc.scalar.activation(out=attn_grouped[:, 0, :, tiles], in_=by_query, func=SIGMOID, scale=-scale)
+
         nc.vector.memset(w_planes[:].rearrange("p g n -> p (g n)").bitcast(I32), 0)
         nc.vector.memset(warm[:], 0.0)
         nc.scalar.activation(out=warm[:, 1:2], in_=warm[:, 0:1], func=SIGMOID)
@@ -244,16 +250,18 @@ def tile_bottleneck_attention_pa_k_kernel(tc, qp_top, kp, v, Wv_words, Wv_scales
 
         for i in range(LOAD_AHEAD):
             load(i)
-        for i in range(SORT_AHEAD):
-            sort_piece(i)
-        short_pieces = len([piece for piece in pieces[:4] if piece[4] == SHORT])
+        sort_piece(0)
+        sort_piece(1)
+        short_pieces = PASSES // SHORT
+        is_sorted = 2
         quantised = 0
         multiplied = 0
         closed = []
         for i in range(n_pieces):
             load(i + LOAD_AHEAD)
             left = transpose_piece(i)
-            while quantised <= i - QUANTISE_BEHIND:
+            at_start = i < short_pieces
+            while quantised <= i - (1 if at_start else QUANTISE_BEHIND):
                 quantise_piece(quantised)
                 quantised += 1
             for j in closed:
@@ -261,42 +269,50 @@ def tile_bottleneck_attention_pa_k_kernel(tc, qp_top, kp, v, Wv_words, Wv_scales
             closed = []
             for dst, src in left:
                 nc.vector.tensor_copy(out=dst, in_=src)
-            sort_piece(i + SORT_AHEAD)
+            while is_sorted <= i + (1 if i + 1 < short_pieces else SORT_AHEAD):
+                sort_piece(is_sorted)
+                is_sorted += 1
             if i == 0:
                 spread_bias()
-            if i < short_pieces or i >= n_pieces - 2 or (i - short_pieces) % 2 == 1:
-                while multiplied <= i - MULTIPLY_BEHIND:
+            if at_start or i >= n_pieces - 2 or (i - short_pieces) % 2 == 1:
+                while multiplied <= i - (1 if at_start else MULTIPLY_BEHIND):
                     multiply_piece(multiplied)
                     closed.append(multiplied)
                     multiplied += 1
         for i in range(quantised, n_pieces):
             quantise_piece(i)
-        for j in closed:
-            finish_row_tile(j)
+            for j in closed:
+                finish_row_tile(j)
+            closed = []
+        softmax(slice(0, ROW_TILES - 1))
         for i in range(multiplied, n_pieces):
             multiply_piece(i)
             finish_row_tile(i)
 
-        scale = 1.0 / math.sqrt(D)
-        by_query = diff[:].rearrange("p t i -> p i t")
-        nc.scalar.activation(out=attn_grouped[:, 1, :, :], in_=by_query, func=SIGMOID, scale=scale)
-        nc.scalar.activation(out=attn_grouped[:, 0, :, :], in_=by_query, func=SIGMOID, scale=-scale)
+        softmax(slice(ROW_TILES - 1, ROW_TILES))
         nc.vector.quantize_mx(
             out=attn_codes[:].bitcast(FP8X4),
             scales=attn_planes[:],
             in_=attn_grouped[:].rearrange("p b i t -> p (b i t)"),
         )
 
-        final = acc_pool.tile([P, BANK_F32], F32, name="acc_v")
-        nc.tensor.matmul_mx(
-            out=final[:],
-            lhsT=attn_codes[:].bitcast(FP8X4),
-            lhsT_scale=attn_planes[:],
-            rhs=vp_codes[:].bitcast(FP8X4),
-            rhs_scale=vp_planes[:],
-            start=True,
-            stop=True,
-        )
-        nc.scalar.copy(out=result[0:BN, :], in_=final[0:BN, 0:DV])
-        nc.vector.tensor_copy(out=result[BN:P, :], in_=final[BN:P, DV : 2 * DV])
+        for b in range(B):
+            if b == 0:
+                final = acc_pool.tile([P, BANK_F32], F32, name="acc_v")
+            else:
+                final = acc_pool.tile([P, BANK_F32], F32, name="acc_kp")
+            cols = slice(b * DV, (b + 1) * DV)
+            nc.tensor.matmul_mx(
+                out=final[:, 0:DV],
+                lhsT=attn_codes[:].bitcast(FP8X4),
+                lhsT_scale=attn_planes[:],
+                rhs=vp_codes[:, cols].bitcast(FP8X4),
+                rhs_scale=vp_planes[:, cols],
+                start=True,
+                stop=True,
+            )
+            if b == 0:
+                nc.scalar.copy(out=result[0:BN, :], in_=final[0:BN, 0:DV])
+            else:
+                nc.vector.tensor_copy(out=result[BN:P, :], in_=final[BN:P, 0:DV])
         nc.sync.dma_start(out=out.rearrange("b i n -> (b i) n"), in_=result[:])

import math
from contextlib import ExitStack

import concourse.mybir as mybir
from concourse.masks import make_identity

BF16 = mybir.dt.bfloat16
F32 = mybir.dt.float32
I32 = mybir.dt.int32
U8 = mybir.dt.uint8
U32 = mybir.dt.uint32
FP8X4 = mybir.dt.float8_e4m3fn_x4
ADD = mybir.AluOpType.add
SUBTRACT = mybir.AluOpType.subtract
SIGMOID = mybir.ActivationFunctionType.Sigmoid

B, L, D, DV, BN = 2, 512, 8192, 256, 64
P = 128
PACK = 4
K_PASS = P * PACK
PASSES = D // K_PASS
ROW_TILES = L // P

LONG, SHORT = 8, 4
SHORT_TILES = 3
V_TILES_FIRST = 6
UNSORTED_TILES = 1
BANK_PASSES = 2
BANK_F32 = 512

RAW_BUFS = 10
LOAD_AHEAD = RAW_BUFS - 1
SORT_AHEAD = 2
QUANTISE_BEHIND = 2
MULTIPLY_BEHIND = 3

FLOPS = 2 * B * L * D * DV + 2 * B * BN * D * L + 2 * B * BN * L * DV


def tile_bottleneck_attention_pa_k_kernel(tc, qp_top, kp, v, Wv_words, Wv_scales, bv, out):
    nc = tc.nc
    with ExitStack() as ctx:
        ctx.enter_context(tc.manual_schedule())
        keep = ctx.enter_context(tc.tile_pool(name="keep", bufs=1))
        raw_pool = ctx.enter_context(tc.tile_pool(name="raw", bufs=RAW_BUFS))
        sorted_pool = ctx.enter_context(tc.tile_pool(name="sorted", bufs=4))
        grouped_pool = ctx.enter_context(tc.tile_pool(name="grouped", bufs=4))
        code_pool = ctx.enter_context(tc.tile_pool(name="codes", bufs=6))
        bank_pool = ctx.enter_context(tc.psum_pool(name="banks", bufs=6))
        acc_pool = ctx.enter_context(tc.psum_pool(name="acc", bufs=1))

        w_codes = keep.tile([P, PASSES, DV * PACK], U8, align_bytes=64)
        w_planes = keep.tile([P, PASSES // SHORT, DV], U8, align_bytes=64)
        q_codes = keep.tile([P, PASSES * P], U32, align_bytes=64)
        q_planes = keep.tile([P, PASSES * P], U8, align_bytes=64)
        ident = keep.tile([P, P], F32)
        ones = keep.tile([P, P], BF16)
        bias_row = keep.tile([P, DV], BF16)
        bias = keep.tile([P, DV], F32)
        score0 = keep.tile([P, ROW_TILES, BN], F32)
        diff = keep.tile([P, ROW_TILES, BN], F32)
        vp_grouped = keep.tile([P, B, DV, PACK], BF16, align_bytes=64)
        vp_codes = keep.tile([P, B * DV], U32, align_bytes=64)
        vp_planes = keep.tile([P, B * DV], U8, align_bytes=64)
        attn_grouped = keep.tile([P, B, BN, PACK], BF16, align_bytes=64)
        attn_codes = keep.tile([P, B * BN], U32, align_bytes=64)
        attn_planes = keep.tile([P, B * BN], U8, align_bytes=64)
        result = keep.tile([P, DV], F32)
        warm = keep.tile([P, 2], F32)

        def cut(kind, tile, size):
            return [(kind, tile // ROW_TILES, tile % ROW_TILES, g, size) for g in range(0, PASSES, size)]

        pieces = []
        for tile in range(V_TILES_FIRST):
            pieces += cut("v", tile, SHORT if tile < SHORT_TILES else LONG)
        pieces += cut("q", 0, LONG)
        rest = [piece for tile in range(V_TILES_FIRST, B * ROW_TILES) for piece in cut("v", tile, LONG)]
        keys = [piece for tile in range(B * ROW_TILES) for piece in cut("kp", tile, LONG)]
        keys = keys[:-1] + cut("kp", B * ROW_TILES - 1, SHORT)[2:]
        for j, piece in enumerate(keys):
            pieces += rest[j : j + 1] + [piece]
        n_pieces = len(pieces)

        words = {}
        groupeds = {}
        codes = {}
        accs = {}

        def load_weight(a):
            g = slice(SHORT * a, SHORT * (a + 1))
            for quadrant in range(4):
                nc.sync.dma_start(
                    out=w_planes[32 * quadrant : 32 * quadrant + 16, a, :].bitcast(I32),
                    in_=Wv_scales[g, 4 * quadrant : 4 * quadrant + 4, :].bitcast(I32),
                )
            nc.sync.dma_start(
                out=w_codes[:, g, :].bitcast(I32),
                in_=Wv_words[g].rearrange("g p n t -> p g (n t)").bitcast(I32),
            )

        def load(i):
            if i >= n_pieces:
                return
            kind, b, t, g, size = pieces[i]
            if kind == "q":
                rows = qp_top.rearrange("b i d -> (b i) d")
            elif kind == "v":
                rows = v[b].rearrange("(p t) d -> t p d", t=ROW_TILES)[t]
            else:
                rows = kp[b].rearrange("(p t) d -> t p d", t=ROW_TILES)[t]
            raw = raw_pool.tile([P, size * K_PASS], BF16, name="raw")
            nc.sync.dma_start(out=raw[:], in_=rows[:, g * K_PASS : (g + size) * K_PASS])
            words[i] = raw[:].bitcast(F32)
            if (kind, b, t) == ("v", 0, 0):
                load_weight(g // SHORT)

        def sort_piece(i):
            if i >= n_pieces or pieces[i][0] != "v" or pieces[i][1] * ROW_TILES + pieces[i][2] < UNSORTED_TILES:
                return
            size = pieces[i][4]
            sorted_words = sorted_pool.tile([P, size * K_PASS // 2], F32, name="sorted_words")
            nc.vector.tensor_copy(
                out=sorted_words[:].rearrange("p (c u w) -> p c u w", u=2, w=P),
                in_=words[i].rearrange("p (c w u) -> p c u w", u=2, w=P),
            )
            words[i] = sorted_words[:]

        def transpose_piece(i):
            kind, b, t, g, size = pieces[i]
            grouped = grouped_pool.tile([P, size * K_PASS], BF16, align_bytes=64, name="grouped")
            groupeds[i] = grouped
            grouped_words = grouped[:].bitcast(F32)
            left = []
            for k in range(size // BANK_PASSES):
                bank = bank_pool.tile([P, BANK_PASSES * 2, P], F32, name="bank")
                for j in range(BANK_PASSES * 2):
                    first = (k * BANK_PASSES * 2 + j) * P
                    block = words[i][:, first : first + P]
                    if kind == "v" and b * ROW_TILES + t < UNSORTED_TILES:
                        first = (k * BANK_PASSES + j // 2) * 2 * P
                        block = words[i][:, first + j % 2 : first + 2 * P : 2]
                    nc.tensor.transpose(bank[:, j, :], block, ident[:])
                src = bank[:].rearrange("p (c u) r -> p c r u", u=2)
                dst = grouped_words[:, k * BANK_F32 : (k + 1) * BANK_F32].rearrange(
                    "p (c r u) -> p c r u", c=BANK_PASSES, u=2
                )
                if kind == "kp" and k == 2:
                    left.append((dst, src))
                else:
                    nc.scalar.copy(out=dst, in_=src)
            return left

        def quantise_piece(i):
            kind, b, t, g, size = pieces[i]
            if kind == "q":
                cols = slice(g * P, (g + size) * P)
                piece_codes, piece_planes = q_codes[:, cols], q_planes[:, cols]
            else:
                code_tile = code_pool.tile([P, size * P], U32, align_bytes=64, name="code_tile")
                plane_tile = code_pool.tile([P, size * P], U8, align_bytes=64, name="plane_tile")
                piece_codes, piece_planes = code_tile[:], plane_tile[:]
            codes[i] = (piece_codes, piece_planes)
            nc.vector.quantize_mx(out=piece_codes.bitcast(FP8X4), scales=piece_planes, in_=groupeds[i][:])

        def multiply_piece(i):
            kind, b, t, g, size = pieces[i]
            if kind == "q":
                return
            if kind == "kp" and g == 0:
                if b * ROW_TILES + t >= B * ROW_TILES - V_TILES_FIRST and (t - V_TILES_FIRST) % 2 == 0:
                    acc_v = acc_pool.tile([P, BANK_F32], F32, name="acc_v")
                    accs[kind, b, t] = acc_v
                else:
                    acc_kp = acc_pool.tile([P, BANK_F32], F32, name="acc_kp")
                    accs[kind, b, t] = acc_kp
            if kind == "v" and g == 0:
                if t % 2 == 1:
                    accs[kind, b, t] = accs[kind, b, t - 1]
                elif (b * ROW_TILES + t) % 4 == 2 and b * ROW_TILES + t < V_TILES_FIRST:
                    acc_kp = acc_pool.tile([P, BANK_F32], F32, name="acc_kp")
                    accs[kind, b, t] = acc_kp
                else:
                    acc_v = acc_pool.tile([P, BANK_F32], F32, name="acc_v")
                    accs[kind, b, t] = acc_v
            acc = accs[kind, b, t]
            left_col = t % 2 * DV if kind == "v" else 0
            piece_codes, piece_planes = codes[i]
            for c in range(size):
                rows = slice(c * P, (c + 1) * P)
                if kind == "v":
                    width = DV
                    rhs, rhs_scale = w_codes[:, g + c, :], w_planes[4 * ((g + c) % SHORT) : P, (g + c) // SHORT, :]
                else:
                    width = B * BN
                    cols = slice((g + c) * P, (g + c + 1) * P)
                    rhs, rhs_scale = q_codes[:, cols], q_planes[:, cols]
                nc.tensor.matmul_mx(
                    out=acc[:, left_col : left_col + width],
                    lhsT=piece_codes[:, rows].bitcast(FP8X4),
                    lhsT_scale=piece_planes[:, rows],
                    rhs=rhs.bitcast(FP8X4),
                    rhs_scale=rhs_scale,
                    start=(g + c == 0),
                    stop=(g + c == PASSES - 1),
                )

        def finish_row_tile(i):
            kind, b, t, g, size = pieces[i]
            if kind == "q" or g + size < PASSES:
                return
            acc = accs[kind, b, t]
            if kind == "v":
                if t % 2 == 1:
                    nc.vector.tensor_tensor(
                        out=vp_grouped[:, b, :, t - 1 : t + 1],
                        in0=acc[:].rearrange("p (j n) -> p n j", j=2),
                        in1=bias[:].unsqueeze(2).to_broadcast([P, DV, 2]),
                        op=ADD,
                    )
                if t == ROW_TILES - 1:
                    nc.vector.quantize_mx(
                        out=vp_codes[:, b * DV : (b + 1) * DV].bitcast(FP8X4),
                        scales=vp_planes[:, b * DV : (b + 1) * DV],
                        in_=vp_grouped[:, b, :, :].rearrange("p n t -> p (n t)"),
                    )
            elif b == 0:
                nc.scalar.copy(out=score0[:, t, :], in_=acc[:, 0:BN])
            else:
                nc.vector.tensor_tensor(out=diff[:, t, :], in0=acc[:, BN : 2 * BN], in1=score0[:, t, :], op=SUBTRACT)

        def softmax(tiles):
            scale = 1.0 / math.sqrt(D)
            by_query = diff[:, tiles, :].rearrange("p t i -> p i t")
            nc.scalar.activation(out=attn_grouped[:, 1, :, tiles], in_=by_query, func=SIGMOID, scale=scale)
            nc.scalar.activation(out=attn_grouped[:, 0, :, tiles], in_=by_query, func=SIGMOID, scale=-scale)

        nc.vector.memset(w_planes[:].rearrange("p g n -> p (g n)").bitcast(I32), 0)
        nc.vector.memset(warm[:], 0.0)
        nc.scalar.activation(out=warm[:, 1:2], in_=warm[:, 0:1], func=SIGMOID)
        make_identity(nc, ident[:])
        nc.gpsimd.memset(ones[:], 1.0)
        nc.gpsimd.memset(bias_row[:], 0.0)
        nc.scalar.dma_start(out=bias_row[0:1, :], in_=bv.rearrange("(o n) -> o n", o=1))

        def spread_bias():
            spread = acc_pool.tile([P, BANK_F32], F32, name="acc_kp")
            nc.tensor.matmul(out=spread[:, 0:DV], lhsT=ones[:], rhs=bias_row[:], start=True, stop=True)
            nc.scalar.copy(out=bias[:], in_=spread[:, 0:DV])

        for i in range(LOAD_AHEAD):
            load(i)
        sort_piece(0)
        sort_piece(1)
        short_pieces = PASSES // SHORT
        is_sorted = 2
        quantised = 0
        multiplied = 0
        closed = []
        for i in range(n_pieces):
            load(i + LOAD_AHEAD)
            left = transpose_piece(i)
            at_start = i < short_pieces
            while quantised <= i - (1 if at_start else QUANTISE_BEHIND):
                quantise_piece(quantised)
                quantised += 1
            for j in closed:
                finish_row_tile(j)
            closed = []
            for dst, src in left:
                nc.vector.tensor_copy(out=dst, in_=src)
            while is_sorted <= i + (1 if i + 1 < short_pieces else SORT_AHEAD):
                sort_piece(is_sorted)
                is_sorted += 1
            if i == 0:
                spread_bias()
            if at_start or i >= n_pieces - 2 or (i - short_pieces) % 2 == 1:
                while multiplied <= i - (1 if at_start else MULTIPLY_BEHIND):
                    multiply_piece(multiplied)
                    closed.append(multiplied)
                    multiplied += 1
        for i in range(quantised, n_pieces):
            quantise_piece(i)
            for j in closed:
                finish_row_tile(j)
            closed = []
        softmax(slice(0, ROW_TILES - 1))
        for i in range(multiplied, n_pieces):
            multiply_piece(i)
            finish_row_tile(i)

        softmax(slice(ROW_TILES - 1, ROW_TILES))
        nc.vector.quantize_mx(
            out=attn_codes[:].bitcast(FP8X4),
            scales=attn_planes[:],
            in_=attn_grouped[:].rearrange("p b i t -> p (b i t)"),
        )

        for b in range(B):
            if b == 0:
                final = acc_pool.tile([P, BANK_F32], F32, name="acc_v")
            else:
                final = acc_pool.tile([P, BANK_F32], F32, name="acc_kp")
            cols = slice(b * DV, (b + 1) * DV)
            nc.tensor.matmul_mx(
                out=final[:, 0:DV],
                lhsT=attn_codes[:].bitcast(FP8X4),
                lhsT_scale=attn_planes[:],
                rhs=vp_codes[:, cols].bitcast(FP8X4),
                rhs_scale=vp_planes[:, cols],
                start=True,
                stop=True,
            )
            if b == 0:
                nc.scalar.copy(out=result[0:BN, :], in_=final[0:BN, 0:DV])
            else:
                nc.vector.tensor_copy(out=result[BN:P, :], in_=final[BN:P, 0:DV])
        nc.sync.dma_start(out=out.rearrange("b i n -> (b i) n"), in_=result[:])
